import numpy as np
import ml_dtypes


def mxq(x, axis, fmt="e4m3"):
    dtype, down = {"e4m3": (ml_dtypes.float8_e4m3fn, 7), "e5m2": (ml_dtypes.float8_e5m2, 14)}[fmt]
    v = np.moveaxis(np.asarray(x, np.float32).astype(ml_dtypes.bfloat16).astype(np.float64), axis, -1)
    blocks = v.reshape(v.shape[:-1] + (-1, 32))
    amax = np.abs(blocks).max(-1, keepdims=True)
    byte = np.maximum(np.where(amax > 0, np.frexp(amax)[1] - 1 + 127, 0) - down, 1)
    scale = np.exp2(byte - 127.0)
    codes = (blocks / scale).astype(np.float32).astype(dtype).astype(np.float64)
    return np.moveaxis((codes * scale).reshape(v.shape), -1, axis)


WIDE = False


def mx_kscale(k):
    if not WIDE:
        return np.ones(k)
    levels = np.array([10, -10, 5, -5, 0])
    a = np.random.permutation(np.resize(levels, k // 512 * 4)).reshape(k // 512, 4)
    idx = np.arange(k)
    return np.exp2(a[idx // 512, idx % 128 // 32])


BF16 = ml_dtypes.bfloat16


def bf(x):
    return np.asarray(x, np.float32).astype(BF16)


def f64(x):
    return np.asarray(x).astype(np.float64)


N, S, K, Yd, Xd = 256, 4, 16, 512, 512
LOG_2PI = np.log(2.0 * np.pi)


def softplus(v):
    return np.maximum(v, 0.0) + np.log(1.0 + np.exp(-np.abs(v)))


def log_softmax(v, axis):
    m = v - v.max(axis, keepdims=True)
    return m - np.log(np.exp(m).sum(axis, keepdims=True))


def mv_gaussian_log_prob(value, mu, sig_diags, event_shape):
    diff = value - mu
    M = np.sum((diff / sig_diags) ** 2, axis=-1)
    half_log_det = np.sum(np.log(sig_diags), axis=-1)
    return -0.5 * (event_shape * LOG_2PI + M) - half_log_det


def setup_inputs():
    s = mx_kscale(Yd)
    return {"Y": bf(np.random.standard_normal((N, Yd)) * 0.5 * s),
            "We_mu": bf(np.random.standard_normal((Yd, Xd)) * 2.0 / np.sqrt(Yd) / s[:, None]),
            "be_mu": bf(np.random.standard_normal(Xd) * 0.1),
            "We_sig": bf(np.random.standard_normal((Yd, Xd)) * 1.0 / np.sqrt(Yd) / s[:, None]),
            "be_sig": bf(-3.0 + np.random.standard_normal(Xd) * 0.1),
            "phi_mus": bf(np.random.standard_normal((K, Xd)) * 3.0 / np.sqrt(Xd)),
            "phi_sigs": bf(1.0 + (np.random.random_sample((K, Xd)) - 0.5) * 9.0 / np.sqrt(Xd)),
            "phi_logits": bf(np.random.standard_normal(K))}


def reference(Y, We_mu, be_mu, We_sig, be_sig, phi_mus, phi_sigs, phi_logits):
    Yq = mxq(f64(Y), 1, "e4m3")
    enc_mu = (Yq @ mxq(f64(We_mu), 0, "e4m3")) + f64(be_mu)
    enc_sig = softplus((Yq @ mxq(f64(We_sig), 0, "e4m3")) + f64(be_sig)) + 1e-3
    log_pi = log_softmax(f64(phi_logits), -1)
    std_k = enc_sig[:, None, :] + f64(phi_sigs)[None, :, :]
    z_logits = log_pi[None, :] + mv_gaussian_log_prob(enc_mu[:, None, :], f64(phi_mus)[None, :, :], std_k, Xd)
    z_log_probs = log_softmax(z_logits, -1)
    return enc_mu, enc_sig, z_log_probs

@@ -1,0 +1,278 @@
+from contextlib import ExitStack
+
+import concourse.masks as masks
+import concourse.mybir as mybir
+
+F32 = mybir.dt.float32
+BF16 = mybir.dt.bfloat16
+U32 = mybir.dt.uint32
+U8 = mybir.dt.uint8
+FP8X4 = mybir.dt.float8_e4m3fn_x4
+ACT = mybir.ActivationFunctionType
+ALU = mybir.AluOpType
+AXIS = mybir.AxisListType
+
+P = 128
+PACK = 4
+ROWS = 256
+Y_DIM = 512
+X_DIM = 512
+CLUSTERS = 16
+NT = ROWS // P
+DT = X_DIM // P
+
+ROW_PHI_MU = 0
+ROW_PHI_SIG = CLUSTERS
+ROW_BE_MU = 2 * CLUSTERS
+ROW_BE_SIG = 2 * CLUSTERS + 1
+PARAM_ROWS = 2 * CLUSTERS + 2
+
+SQUARE_PERIOD = 8
+SQUARE_ON_SCALAR = 3
+LEAD = 2
+
+FLOPS = 2 * 2 * ROWS * Y_DIM * X_DIM
+
+
+def tile_deepgmm_pa_s_kernel(
+    tc, Y, We_mu, be_mu, We_sig, be_sig, phi_mus, phi_sigs, phi_logits, out_0, out_1, out_2
+):
+    nc = tc.nc
+    with ExitStack() as ctx:
+        keep = ctx.enter_context(tc.tile_pool(name="keep", bufs=1))
+        work = ctx.enter_context(tc.tile_pool(name="work", bufs=3))
+        psum = ctx.enter_context(tc.psum_pool(name="psum", bufs=8))
+        ctx.enter_context(tc.manual_schedule())
+
+        ident = keep.tile([P, P], F32)
+        masks.make_identity(nc, ident[:])
+        one_col = keep.tile([P, 1], F32)
+        nc.vector.memset(one_col[:], 1.0)
+        param_rows = keep.tile([P, X_DIM], BF16)
+        nc.vector.memset(param_rows[:], 0.0)
+
+        y_sb = keep.tile([P, NT, Y_DIM], BF16)
+        nc.sync.dma_start(out=y_sb[:], in_=Y.rearrange("(t p) k -> p t k", p=P))
+
+        def load_weight(raw, w):
+            nc.sync.dma_start(
+                out=raw[:].rearrange("p (u e) c -> p u (e c)", u=2),
+                in_=w.rearrange("(u p e) c -> p u (e c)", u=2, e=2),
+            )
+
+        wsig_raw = keep.tile([P, PACK, X_DIM], BF16)
+        load_weight(wsig_raw, We_sig)
+        wmu_raw = keep.tile([P, PACK, X_DIM], BF16)
+        load_weight(wmu_raw, We_mu)
+
+        nc.scalar.dma_start(out=param_rows[ROW_PHI_SIG : ROW_PHI_SIG + CLUSTERS, :], in_=phi_sigs)
+        nc.scalar.dma_start(out=param_rows[ROW_PHI_MU : ROW_PHI_MU + CLUSTERS, :], in_=phi_mus)
+        nc.scalar.dma_start(
+            out=param_rows[ROW_BE_SIG : ROW_BE_SIG + 1, :], in_=be_sig.rearrange("(o d) -> o d", o=1)
+        )
+        nc.scalar.dma_start(
+            out=param_rows[ROW_BE_MU : ROW_BE_MU + 1, :], in_=be_mu.rearrange("(o d) -> o d", o=1)
+        )
+        logits = keep.tile([P, CLUSTERS], BF16)
+        nc.scalar.dma_start(out=logits[:], in_=phi_logits.partition_broadcast(P))
+
+        warm = keep.tile([P, 1], F32)
+        nc.scalar.activation(out=warm[:], in_=one_col[:], func=ACT.Exp)
+
+        y_words = y_sb[:].bitcast(F32)
+        yT_ps = psum.tile([P, 2, ROWS], F32, tag="bank")
+        for nt in range(NT):
+            for u in range(2):
+                nc.tensor.transpose(
+                    yT_ps[:, u, nt * P : (nt + 1) * P], y_words[:, nt, u * P : (u + 1) * P], ident[:]
+                )
+        y_grouped = keep.tile([P, ROWS, PACK], BF16, align_bytes=64)
+        nc.vector.tensor_copy(
+            out=y_grouped[:].bitcast(F32), in_=yT_ps[:].rearrange("p u n -> p n u")
+        )
+
+        param_rows_f = keep.tile([P, X_DIM], F32)
+        nc.scalar.copy(out=param_rows_f[:], in_=param_rows[:])
+        param_ps = psum.tile([P, DT, P], F32, tag="bank")
+        for dt in range(DT):
+            nc.tensor.transpose(param_ps[:, dt, :], param_rows_f[:, dt * P : (dt + 1) * P], ident[:])
+        params = keep.tile([P, DT, PARAM_ROWS], F32)
+        nc.scalar.copy(out=params[:], in_=param_ps[:, :, 0:PARAM_ROWS])
+
+        def param(dt, row):
+            return params[:, dt, row : row + 1]
+
+        def group(copy, grouped, raw):
+            copy(
+                out=grouped[:].rearrange("p (c i) t -> p c t i", i=4),
+                in_=raw[:].rearrange("p t (c i) -> p c t i", i=4),
+            )
+
+        def quantise(codes, scales, grouped):
+            nc.vector.quantize_mx(
+                out=codes[:].bitcast(FP8X4),
+                scales=scales[:],
+                in_=grouped[:].rearrange("p c t -> p (c t)"),
+            )
+
+        wsig_grouped = keep.tile([P, X_DIM, PACK], BF16, align_bytes=64)
+        group(nc.vector.tensor_copy, wsig_grouped, wsig_raw)
+        wmu_grouped = keep.tile([P, X_DIM, PACK], BF16, align_bytes=64)
+        group(nc.scalar.copy, wmu_grouped, wmu_raw)
+
+        y_codes = keep.tile([P, ROWS], U32, align_bytes=64)
+        y_scales = keep.tile([P, ROWS], U8, align_bytes=64)
+        quantise(y_codes, y_scales, y_grouped)
+        wsig_codes = keep.tile([P, X_DIM], U32, align_bytes=64)
+        wsig_scales = keep.tile([P, X_DIM], U8, align_bytes=64)
+        quantise(wsig_codes, wsig_scales, wsig_grouped)
+
+        def project(w_codes, w_scales):
+            banks = []
+            for half in range(DT // 2):
+                acc = psum.tile([P, 2, ROWS], F32, tag="bank", name="acc")
+                for j in range(2):
+                    cols = slice((2 * half + j) * P, (2 * half + j + 1) * P)
+                    nc.tensor.matmul_mx(
+                        out=acc[:, j, :],
+                        lhsT=w_codes[:, cols].bitcast(FP8X4),
+                        lhsT_scale=w_scales[:, cols],
+                        rhs=y_codes[:].bitcast(FP8X4),
+                        rhs_scale=y_scales[:],
+                        start=True,
+                        stop=True,
+                    )
+                banks.append(acc)
+            return banks
+
+        sig_banks = project(wsig_codes, wsig_scales)
+        v = keep.tile([P, DT, ROWS], F32)
+        term = keep.tile([P, DT, ROWS], F32)
+        for dt in range(DT):
+            nc.vector.tensor_scalar(
+                out=v[:, dt, :], in0=sig_banks[dt // 2][:, dt % 2, :],
+                scalar1=param(dt, ROW_BE_SIG), scalar2=None, op0=ALU.add,
+            )
+            nc.scalar.activation(out=term[:, dt, :], in_=v[:, dt, :], func=ACT.Abs)
+        nc.scalar.activation(out=term[:], in_=term[:], func=ACT.Exp, scale=-1.0)
+        for dt in range(DT):
+            nc.scalar.activation(out=term[:, dt, :], in_=term[:, dt, :], func=ACT.Ln, bias=one_col[:])
+
+        wmu_codes = keep.tile([P, X_DIM], U32, align_bytes=64)
+        wmu_scales = keep.tile([P, X_DIM], U8, align_bytes=64)
+        quantise(wmu_codes, wmu_scales, wmu_grouped)
+        mu_banks = project(wmu_codes, wmu_scales)
+        muT = keep.tile([P, DT, ROWS], F32)
+        for dt in range(DT):
+            nc.vector.tensor_scalar(
+                out=muT[:, dt, :], in0=mu_banks[dt // 2][:, dt % 2, :],
+                scalar1=param(dt, ROW_BE_MU), scalar2=None, op0=ALU.add,
+            )
+        relu_v = keep.tile([P, DT, ROWS], F32)
+        nc.vector.tensor_scalar_max(out=relu_v[:], in0=v[:], scalar1=0.0)
+
+        dist2 = keep.tile([P, CLUSTERS, DT, ROWS], F32)
+
+        def squared_distance(k):
+            for dt in range(DT):
+                if (k * DT + dt) % SQUARE_PERIOD < SQUARE_ON_SCALAR:
+                    nc.scalar.activation(
+                        out=dist2[:, k, dt, :], in_=muT[:, dt, :], func=ACT.Square,
+                        scale=-1.0, bias=param(dt, ROW_PHI_MU + k),
+                    )
+                else:
+                    diff = work.tile([P, ROWS], F32)
+                    nc.vector.tensor_scalar(
+                        out=diff[:], in0=muT[:, dt, :],
+                        scalar1=param(dt, ROW_PHI_MU + k), scalar2=None, op0=ALU.subtract,
+                    )
+                    nc.vector.tensor_tensor(out=dist2[:, k, dt, :], in0=diff[:], in1=diff[:], op=ALU.mult)
+
+        for k in range(LEAD):
+            squared_distance(k)
+
+        sigT = keep.tile([P, DT, ROWS], F32)
+        for dt in range(DT):
+            nc.vector.scalar_tensor_tensor(
+                out=sigT[:, dt, :], in0=term[:, dt, :], scalar=1e-3, in1=relu_v[:, dt, :],
+                op0=ALU.add, op1=ALU.add,
+            )
+
+        def rows_onto_partitions(src):
+            bank = psum.tile([P, X_DIM], F32, tag="bank", name="bank")
+            for dt in range(DT):
+                nc.tensor.transpose(bank[:, dt * P : (dt + 1) * P], src[:, dt, :], ident[:])
+            return bank
+
+        ln_std = keep.tile([P, CLUSTERS, NT, X_DIM], F32)
+        ln_sum = keep.tile([P, NT, CLUSTERS], F32)
+        for k in range(CLUSTERS):
+            stdT = work.tile([P, DT, ROWS], F32)
+            for dt in range(DT):
+                nc.vector.tensor_scalar(
+                    out=stdT[:, dt, :], in0=sigT[:, dt, :],
+                    scalar1=param(dt, ROW_PHI_SIG + k), scalar2=None, op0=ALU.add,
+                )
+            for nt in range(NT):
+                std = rows_onto_partitions(stdT[:, :, nt * P : (nt + 1) * P])
+                nc.scalar.activation(
+                    out=ln_std[:, k, nt, :], in_=std[:], func=ACT.Ln,
+                    accum_out=ln_sum[:, nt, k : k + 1],
+                )
+            if k + LEAD < CLUSTERS:
+                squared_distance(k + LEAD)
+
+        base = keep.tile([P, NT, CLUSTERS], F32)
+        nc.vector.tensor_tensor(
+            out=base[:], in0=logits[:].unsqueeze(1).to_broadcast([P, NT, CLUSTERS]), in1=ln_sum[:],
+            op=ALU.subtract,
+        )
+
+        maha_sum = keep.tile([P, NT, CLUSTERS], F32)
+        for k in range(CLUSTERS):
+            inv_var = work.tile([P, NT, X_DIM], F32)
+            nc.scalar.activation(out=inv_var[:], in_=ln_std[:, k, :, :], func=ACT.Exp, scale=-2.0)
+            for nt in range(NT):
+                d2 = rows_onto_partitions(dist2[:, k, :, nt * P : (nt + 1) * P])
+                product = work.tile([P, X_DIM], F32)
+                nc.vector.scalar_tensor_tensor(
+                    out=product[:], in0=d2[:], scalar=0.5, in1=inv_var[:, nt, :],
+                    op0=ALU.mult, op1=ALU.mult, accum_out=maha_sum[:, nt, k : k + 1],
+                )
+
+        def store_rows(copy, dram, src):
+            for nt in range(NT):
+                bank = rows_onto_partitions(src[:, :, nt * P : (nt + 1) * P])
+                rows_sb = work.tile([P, X_DIM], F32)
+                copy(out=rows_sb[:], in_=bank[:])
+                nc.sync.dma_start(out=dram[nt * P : (nt + 1) * P, :], in_=rows_sb[:])
+
+        store_rows(nc.scalar.copy, out_0, muT)
+
+        z = keep.tile([P, NT, CLUSTERS], F32)
+        nc.vector.tensor_tensor(out=z[:], in0=base[:], in1=maha_sum[:], op=ALU.subtract)
+        z_max = keep.tile([P, NT], F32)
+        nc.vector.tensor_reduce(out=z_max[:], in_=z[:], axis=AXIS.X, op=ALU.max)
+        z_shift = keep.tile([P, NT, CLUSTERS], F32)
+        nc.vector.tensor_tensor(
+            out=z_shift[:], in0=z[:], in1=z_max[:].unsqueeze(2).to_broadcast([P, NT, CLUSTERS]),
+            op=ALU.subtract,
+        )
+        exp_z = keep.tile([P, NT, CLUSTERS], F32)
+        exp_sum = keep.tile([P, NT], F32)
+        for nt in range(NT):
+            nc.scalar.activation(
+                out=exp_z[:, nt, :], in_=z_shift[:, nt, :], func=ACT.Exp,
+                accum_out=exp_sum[:, nt : nt + 1],
+            )
+        log_sum = keep.tile([P, NT], F32)
+        nc.scalar.activation(out=log_sum[:], in_=exp_sum[:], func=ACT.Ln)
+
+        store_rows(nc.vector.tensor_copy, out_1, sigT)
+
+        z_log_probs = keep.tile([P, NT, CLUSTERS], F32)
+        nc.vector.tensor_tensor(
+            out=z_log_probs[:], in0=z_shift[:],
+            in1=log_sum[:].unsqueeze(2).to_broadcast([P, NT, CLUSTERS]), op=ALU.subtract,
+        )
+        nc.sync.dma_start(out=out_2.rearrange("(t p) k -> p t k", p=P), in_=z_log_probs[:])

@@ -27,9 +27,11 @@ ROW_BE_MU = 2 * CLUSTERS
 ROW_BE_SIG = 2 * CLUSTERS + 1
 PARAM_ROWS = 2 * CLUSTERS + 2
 
-SQUARE_PERIOD = 8
-SQUARE_ON_SCALAR = 3
-LEAD = 2
+VECTOR_CLUSTERS = 10
+HALF = DT // 2
+VECTOR_UNITS = VECTOR_CLUSTERS * DT // HALF
+SCALAR_UNITS = (CLUSTERS - VECTOR_CLUSTERS) * DT
+SCALAR_LEAD = SCALAR_UNITS - CLUSTERS
 
 FLOPS = 2 * 2 * ROWS * Y_DIM * X_DIM
 
@@ -118,7 +120,6 @@ def tile_deepgmm_pa_s_kernel(
         wsig_grouped = keep.tile([P, X_DIM, PACK], BF16, align_bytes=64)
         group(nc.vector.tensor_copy, wsig_grouped, wsig_raw)
         wmu_grouped = keep.tile([P, X_DIM, PACK], BF16, align_bytes=64)
-        group(nc.scalar.copy, wmu_grouped, wmu_raw)
 
         y_codes = keep.tile([P, ROWS], U32, align_bytes=64)
         y_scales = keep.tile([P, ROWS], U8, align_bytes=64)
@@ -126,6 +127,7 @@ def tile_deepgmm_pa_s_kernel(
         wsig_codes = keep.tile([P, X_DIM], U32, align_bytes=64)
         wsig_scales = keep.tile([P, X_DIM], U8, align_bytes=64)
         quantise(wsig_codes, wsig_scales, wsig_grouped)
+        group(nc.vector.tensor_copy, wmu_grouped, wmu_raw)
 
         def project(w_codes, w_scales):
             banks = []
@@ -173,23 +175,27 @@ def tile_deepgmm_pa_s_kernel(
 
         dist2 = keep.tile([P, CLUSTERS, DT, ROWS], F32)
 
-        def squared_distance(k):
-            for dt in range(DT):
-                if (k * DT + dt) % SQUARE_PERIOD < SQUARE_ON_SCALAR:
-                    nc.scalar.activation(
-                        out=dist2[:, k, dt, :], in_=muT[:, dt, :], func=ACT.Square,
-                        scale=-1.0, bias=param(dt, ROW_PHI_MU + k),
-                    )
-                else:
-                    diff = work.tile([P, ROWS], F32)
-                    nc.vector.tensor_scalar(
-                        out=diff[:], in0=muT[:, dt, :],
-                        scalar1=param(dt, ROW_PHI_MU + k), scalar2=None, op0=ALU.subtract,
-                    )
-                    nc.vector.tensor_tensor(out=dist2[:, k, dt, :], in0=diff[:], in1=diff[:], op=ALU.mult)
+        def vector_square(unit):
+            k, half = divmod(unit, DT // HALF)
+            tiles = slice(half * HALF, (half + 1) * HALF)
+            diff = work.tile([P, HALF, ROWS], F32)
+            for j in range(HALF):
+                dt = half * HALF + j
+                nc.vector.tensor_scalar(
+                    out=diff[:, j, :], in0=muT[:, dt, :],
+                    scalar1=param(dt, ROW_PHI_MU + k), scalar2=None, op0=ALU.subtract,
+                )
+            nc.vector.tensor_tensor(out=dist2[:, k, tiles, :], in0=diff[:], in1=diff[:], op=ALU.mult)
 
-        for k in range(LEAD):
-            squared_distance(k)
+        def scalar_square(unit):
+            k, dt = divmod(VECTOR_CLUSTERS * DT + unit, DT)
+            nc.scalar.activation(
+                out=dist2[:, k, dt, :], in_=muT[:, dt, :], func=ACT.Square,
+                scale=-1.0, bias=param(dt, ROW_PHI_MU + k),
+            )
+
+        for unit in range(SCALAR_LEAD):
+            scalar_square(unit)
 
         sigT = keep.tile([P, DT, ROWS], F32)
         for dt in range(DT):
@@ -219,8 +225,10 @@ def tile_deepgmm_pa_s_kernel(
                     out=ln_std[:, k, nt, :], in_=std[:], func=ACT.Ln,
                     accum_out=ln_sum[:, nt, k : k + 1],
                 )
-            if k + LEAD < CLUSTERS:
-                squared_distance(k + LEAD)
+            scalar_square(SCALAR_LEAD + k)
+            vector_square(k)
+        for unit in range(CLUSTERS, VECTOR_UNITS):
+            vector_square(unit)
 
         base = keep.tile([P, NT, CLUSTERS], F32)
         nc.vector.tensor_tensor(

@@ -43,6 +43,7 @@ def tile_deepgmm_pa_s_kernel(
     with ExitStack() as ctx:
         keep = ctx.enter_context(tc.tile_pool(name="keep", bufs=1))
         work = ctx.enter_context(tc.tile_pool(name="work", bufs=3))
+        diffs = ctx.enter_context(tc.tile_pool(name="diffs", bufs=VECTOR_UNITS - CLUSTERS))
         psum = ctx.enter_context(tc.psum_pool(name="psum", bufs=8))
         ctx.enter_context(tc.manual_schedule())
 
@@ -66,6 +67,8 @@ def tile_deepgmm_pa_s_kernel(
         load_weight(wsig_raw, We_sig)
         wmu_raw = keep.tile([P, PACK, X_DIM], BF16)
         load_weight(wmu_raw, We_mu)
+        logits = keep.tile([P, CLUSTERS], BF16)
+        nc.sync.dma_start(out=logits[:], in_=phi_logits.partition_broadcast(P))
 
         nc.scalar.dma_start(out=param_rows[ROW_PHI_SIG : ROW_PHI_SIG + CLUSTERS, :], in_=phi_sigs)
         nc.scalar.dma_start(out=param_rows[ROW_PHI_MU : ROW_PHI_MU + CLUSTERS, :], in_=phi_mus)
@@ -75,8 +78,6 @@ def tile_deepgmm_pa_s_kernel(
         nc.scalar.dma_start(
             out=param_rows[ROW_BE_MU : ROW_BE_MU + 1, :], in_=be_mu.rearrange("(o d) -> o d", o=1)
         )
-        logits = keep.tile([P, CLUSTERS], BF16)
-        nc.scalar.dma_start(out=logits[:], in_=phi_logits.partition_broadcast(P))
 
         warm = keep.tile([P, 1], F32)
         nc.scalar.activation(out=warm[:], in_=one_col[:], func=ACT.Exp)
@@ -156,7 +157,8 @@ def tile_deepgmm_pa_s_kernel(
                 scalar1=param(dt, ROW_BE_SIG), scalar2=None, op0=ALU.add,
             )
             nc.scalar.activation(out=term[:, dt, :], in_=v[:, dt, :], func=ACT.Abs)
-        nc.scalar.activation(out=term[:], in_=term[:], func=ACT.Exp, scale=-1.0)
+        for dt in range(DT):
+            nc.scalar.activation(out=term[:, dt, :], in_=term[:, dt, :], func=ACT.Exp, scale=-1.0)
         for dt in range(DT):
             nc.scalar.activation(out=term[:, dt, :], in_=term[:, dt, :], func=ACT.Ln, bias=one_col[:])
 
@@ -175,16 +177,20 @@ def tile_deepgmm_pa_s_kernel(
 
         dist2 = keep.tile([P, CLUSTERS, DT, ROWS], F32)
 
-        def vector_square(unit):
+        def vector_difference(unit):
             k, half = divmod(unit, DT // HALF)
-            tiles = slice(half * HALF, (half + 1) * HALF)
-            diff = work.tile([P, HALF, ROWS], F32)
+            diff = diffs.tile([P, HALF, ROWS], F32)
             for j in range(HALF):
                 dt = half * HALF + j
                 nc.vector.tensor_scalar(
                     out=diff[:, j, :], in0=muT[:, dt, :],
                     scalar1=param(dt, ROW_PHI_MU + k), scalar2=None, op0=ALU.subtract,
                 )
+            return diff
+
+        def vector_square(unit, diff):
+            k, half = divmod(unit, DT // HALF)
+            tiles = slice(half * HALF, (half + 1) * HALF)
             nc.vector.tensor_tensor(out=dist2[:, k, tiles, :], in0=diff[:], in1=diff[:], op=ALU.mult)
 
         def scalar_square(unit):
@@ -213,6 +219,7 @@ def tile_deepgmm_pa_s_kernel(
         ln_std = keep.tile([P, CLUSTERS, NT, X_DIM], F32)
         ln_sum = keep.tile([P, NT, CLUSTERS], F32)
         for k in range(CLUSTERS):
+            diff = vector_difference(k)
             stdT = work.tile([P, DT, ROWS], F32)
             for dt in range(DT):
                 nc.vector.tensor_scalar(
@@ -226,9 +233,11 @@ def tile_deepgmm_pa_s_kernel(
                     accum_out=ln_sum[:, nt, k : k + 1],
                 )
             scalar_square(SCALAR_LEAD + k)
-            vector_square(k)
-        for unit in range(CLUSTERS, VECTOR_UNITS):
-            vector_square(unit)
+            vector_square(k, diff)
+        rest = range(CLUSTERS, VECTOR_UNITS)
+        rest_diffs = [vector_difference(unit) for unit in rest]
+        for unit, diff in zip(rest, rest_diffs):
+            vector_square(unit, diff)
 
         base = keep.tile([P, NT, CLUSTERS], F32)
         nc.vector.tensor_tensor(

@@ -27,11 +27,16 @@ ROW_BE_MU = 2 * CLUSTERS
 ROW_BE_SIG = 2 * CLUSTERS + 1
 PARAM_ROWS = 2 * CLUSTERS + 2
 
-VECTOR_CLUSTERS = 10
+VECTOR_CLUSTERS = 8
+SCALAR_CLUSTERS = 5
 HALF = DT // 2
-VECTOR_UNITS = VECTOR_CLUSTERS * DT // HALF
-SCALAR_UNITS = (CLUSTERS - VECTOR_CLUSTERS) * DT
-SCALAR_LEAD = SCALAR_UNITS - CLUSTERS
+UNITS_PER_CLUSTER = DT // HALF
+VECTOR_UNITS = VECTOR_CLUSTERS * UNITS_PER_CLUSTER
+GPSIMD_FIRST_UNIT = (VECTOR_CLUSTERS + SCALAR_CLUSTERS) * UNITS_PER_CLUSTER
+ALL_UNITS = CLUSTERS * UNITS_PER_CLUSTER
+VECTOR_START = 4
+SCALAR_UNITS = SCALAR_CLUSTERS * DT
+SCALAR_LEAD = SCALAR_UNITS // 2
 
 FLOPS = 2 * 2 * ROWS * Y_DIM * X_DIM
 
@@ -43,7 +48,8 @@ def tile_deepgmm_pa_s_kernel(
     with ExitStack() as ctx:
         keep = ctx.enter_context(tc.tile_pool(name="keep", bufs=1))
         work = ctx.enter_context(tc.tile_pool(name="work", bufs=3))
-        diffs = ctx.enter_context(tc.tile_pool(name="diffs", bufs=VECTOR_UNITS - CLUSTERS))
+        outs = ctx.enter_context(tc.tile_pool(name="outs", bufs=2 * NT))
+        diffs = ctx.enter_context(tc.tile_pool(name="diffs", bufs=VECTOR_UNITS - (CLUSTERS - VECTOR_START)))
         psum = ctx.enter_context(tc.psum_pool(name="psum", bufs=8))
         ctx.enter_context(tc.manual_schedule())
 
@@ -178,7 +184,7 @@ def tile_deepgmm_pa_s_kernel(
         dist2 = keep.tile([P, CLUSTERS, DT, ROWS], F32)
 
         def vector_difference(unit):
-            k, half = divmod(unit, DT // HALF)
+            k, half = divmod(unit, UNITS_PER_CLUSTER)
             diff = diffs.tile([P, HALF, ROWS], F32)
             for j in range(HALF):
                 dt = half * HALF + j
@@ -188,10 +194,21 @@ def tile_deepgmm_pa_s_kernel(
                 )
             return diff
 
-        def vector_square(unit, diff):
-            k, half = divmod(unit, DT // HALF)
+        def square(engine, unit, diff):
+            k, half = divmod(unit, UNITS_PER_CLUSTER)
             tiles = slice(half * HALF, (half + 1) * HALF)
-            nc.vector.tensor_tensor(out=dist2[:, k, tiles, :], in0=diff[:], in1=diff[:], op=ALU.mult)
+            engine.tensor_tensor(out=dist2[:, k, tiles, :], in0=diff[:], in1=diff[:], op=ALU.mult)
+
+        def gpsimd_square(unit):
+            k, half = divmod(unit, UNITS_PER_CLUSTER)
+            diff = diffs.tile([P, HALF, ROWS], F32)
+            for j in range(HALF):
+                dt = half * HALF + j
+                nc.gpsimd.tensor_scalar(
+                    out=diff[:, j, :], in0=muT[:, dt, :],
+                    scalar1=-1.0, scalar2=param(dt, ROW_PHI_MU + k), op0=ALU.mult, op1=ALU.add,
+                )
+            square(nc.gpsimd, unit, diff)
 
         def scalar_square(unit):
             k, dt = divmod(VECTOR_CLUSTERS * DT + unit, DT)
@@ -219,7 +236,8 @@ def tile_deepgmm_pa_s_kernel(
         ln_std = keep.tile([P, CLUSTERS, NT, X_DIM], F32)
         ln_sum = keep.tile([P, NT, CLUSTERS], F32)
         for k in range(CLUSTERS):
-            diff = vector_difference(k)
+            if k >= VECTOR_START:
+                diff = vector_difference(k - VECTOR_START)
             stdT = work.tile([P, DT, ROWS], F32)
             for dt in range(DT):
                 nc.vector.tensor_scalar(
@@ -232,12 +250,14 @@ def tile_deepgmm_pa_s_kernel(
                     out=ln_std[:, k, nt, :], in_=std[:], func=ACT.Ln,
                     accum_out=ln_sum[:, nt, k : k + 1],
                 )
-            scalar_square(SCALAR_LEAD + k)
-            vector_square(k, diff)
-        rest = range(CLUSTERS, VECTOR_UNITS)
+            if k >= VECTOR_START:
+                square(nc.vector, k - VECTOR_START, diff)
+        rest = range(CLUSTERS - VECTOR_START, VECTOR_UNITS)
         rest_diffs = [vector_difference(unit) for unit in rest]
         for unit, diff in zip(rest, rest_diffs):
-            vector_square(unit, diff)
+            square(nc.vector, unit, diff)
+        for unit in range(GPSIMD_FIRST_UNIT, ALL_UNITS):
+            gpsimd_square(unit)
 
         base = keep.tile([P, NT, CLUSTERS], F32)
         nc.vector.tensor_tensor(
@@ -249,6 +269,8 @@ def tile_deepgmm_pa_s_kernel(
         for k in range(CLUSTERS):
             inv_var = work.tile([P, NT, X_DIM], F32)
             nc.scalar.activation(out=inv_var[:], in_=ln_std[:, k, :, :], func=ACT.Exp, scale=-2.0)
+            if SCALAR_LEAD + k < SCALAR_UNITS:
+                scalar_square(SCALAR_LEAD + k)
             for nt in range(NT):
                 d2 = rows_onto_partitions(dist2[:, k, :, nt * P : (nt + 1) * P])
                 product = work.tile([P, X_DIM], F32)
@@ -260,7 +282,7 @@ def tile_deepgmm_pa_s_kernel(
         def store_rows(copy, dram, src):
             for nt in range(NT):
                 bank = rows_onto_partitions(src[:, :, nt * P : (nt + 1) * P])
-                rows_sb = work.tile([P, X_DIM], F32)
+                rows_sb = outs.tile([P, X_DIM], F32)
                 copy(out=rows_sb[:], in_=bank[:])
                 nc.sync.dma_start(out=dram[nt * P : (nt + 1) * P, :], in_=rows_sb[:])
 

@@ -13,13 +13,23 @@ ALU = mybir.AluOpType
 AXIS = mybir.AxisListType
 
 P = 128
-PACK = 4
+PSUM_BANKS = 8
+BANK_F32 = 512
+
 ROWS = 256
 Y_DIM = 512
 X_DIM = 512
 CLUSTERS = 16
+SIG_FLOOR = 1e-3
 NT = ROWS // P
 DT = X_DIM // P
+
+PACK = 4
+PAIR = 2
+HALVES = PACK // PAIR
+assert Y_DIM == P * PACK
+RUN = 4
+TILES_PER_BANK = BANK_F32 // ROWS
 
 ROW_PHI_MU = 0
 ROW_PHI_SIG = CLUSTERS
@@ -34,7 +44,8 @@ UNITS_PER_CLUSTER = DT // HALF
 VECTOR_UNITS = VECTOR_CLUSTERS * UNITS_PER_CLUSTER
 GPSIMD_FIRST_UNIT = (VECTOR_CLUSTERS + SCALAR_CLUSTERS) * UNITS_PER_CLUSTER
 ALL_UNITS = CLUSTERS * UNITS_PER_CLUSTER
-VECTOR_START = 4
+VECTOR_START = PSUM_BANKS // NT
+VECTOR_REST = VECTOR_UNITS - (CLUSTERS - VECTOR_START)
 SCALAR_UNITS = SCALAR_CLUSTERS * DT
 SCALAR_LEAD = SCALAR_UNITS // 2
 
@@ -47,74 +58,19 @@ def tile_deepgmm_pa_s_kernel(
     nc = tc.nc
     with ExitStack() as ctx:
         keep = ctx.enter_context(tc.tile_pool(name="keep", bufs=1))
-        work = ctx.enter_context(tc.tile_pool(name="work", bufs=3))
-        outs = ctx.enter_context(tc.tile_pool(name="outs", bufs=2 * NT))
-        diffs = ctx.enter_context(tc.tile_pool(name="diffs", bufs=VECTOR_UNITS - (CLUSTERS - VECTOR_START)))
-        psum = ctx.enter_context(tc.psum_pool(name="psum", bufs=8))
+        psum = ctx.enter_context(tc.psum_pool(name="psum", bufs=PSUM_BANKS))
         ctx.enter_context(tc.manual_schedule())
-
-        ident = keep.tile([P, P], F32)
-        masks.make_identity(nc, ident[:])
-        one_col = keep.tile([P, 1], F32)
-        nc.vector.memset(one_col[:], 1.0)
-        param_rows = keep.tile([P, X_DIM], BF16)
-        nc.vector.memset(param_rows[:], 0.0)
-
-        y_sb = keep.tile([P, NT, Y_DIM], BF16)
-        nc.sync.dma_start(out=y_sb[:], in_=Y.rearrange("(t p) k -> p t k", p=P))
 
         def load_weight(raw, w):
             nc.sync.dma_start(
-                out=raw[:].rearrange("p (u e) c -> p u (e c)", u=2),
-                in_=w.rearrange("(u p e) c -> p u (e c)", u=2, e=2),
+                out=raw[:].rearrange("p (u e) c -> p u (e c)", u=HALVES),
+                in_=w.rearrange("(u p e) c -> p u (e c)", u=HALVES, e=PAIR),
             )
 
-        wsig_raw = keep.tile([P, PACK, X_DIM], BF16)
-        load_weight(wsig_raw, We_sig)
-        wmu_raw = keep.tile([P, PACK, X_DIM], BF16)
-        load_weight(wmu_raw, We_mu)
-        logits = keep.tile([P, CLUSTERS], BF16)
-        nc.sync.dma_start(out=logits[:], in_=phi_logits.partition_broadcast(P))
-
-        nc.scalar.dma_start(out=param_rows[ROW_PHI_SIG : ROW_PHI_SIG + CLUSTERS, :], in_=phi_sigs)
-        nc.scalar.dma_start(out=param_rows[ROW_PHI_MU : ROW_PHI_MU + CLUSTERS, :], in_=phi_mus)
-        nc.scalar.dma_start(
-            out=param_rows[ROW_BE_SIG : ROW_BE_SIG + 1, :], in_=be_sig.rearrange("(o d) -> o d", o=1)
-        )
-        nc.scalar.dma_start(
-            out=param_rows[ROW_BE_MU : ROW_BE_MU + 1, :], in_=be_mu.rearrange("(o d) -> o d", o=1)
-        )
-
-        warm = keep.tile([P, 1], F32)
-        nc.scalar.activation(out=warm[:], in_=one_col[:], func=ACT.Exp)
-
-        y_words = y_sb[:].bitcast(F32)
-        yT_ps = psum.tile([P, 2, ROWS], F32, tag="bank")
-        for nt in range(NT):
-            for u in range(2):
-                nc.tensor.transpose(
-                    yT_ps[:, u, nt * P : (nt + 1) * P], y_words[:, nt, u * P : (u + 1) * P], ident[:]
-                )
-        y_grouped = keep.tile([P, ROWS, PACK], BF16, align_bytes=64)
-        nc.vector.tensor_copy(
-            out=y_grouped[:].bitcast(F32), in_=yT_ps[:].rearrange("p u n -> p n u")
-        )
-
-        param_rows_f = keep.tile([P, X_DIM], F32)
-        nc.scalar.copy(out=param_rows_f[:], in_=param_rows[:])
-        param_ps = psum.tile([P, DT, P], F32, tag="bank")
-        for dt in range(DT):
-            nc.tensor.transpose(param_ps[:, dt, :], param_rows_f[:, dt * P : (dt + 1) * P], ident[:])
-        params = keep.tile([P, DT, PARAM_ROWS], F32)
-        nc.scalar.copy(out=params[:], in_=param_ps[:, :, 0:PARAM_ROWS])
-
-        def param(dt, row):
-            return params[:, dt, row : row + 1]
-
-        def group(copy, grouped, raw):
-            copy(
-                out=grouped[:].rearrange("p (c i) t -> p c t i", i=4),
-                in_=raw[:].rearrange("p t (c i) -> p c t i", i=4),
+        def group(grouped, raw):
+            nc.vector.tensor_copy(
+                out=grouped[:].rearrange("p (c i) t -> p c t i", i=RUN),
+                in_=raw[:].rearrange("p t (c i) -> p c t i", i=RUN),
             )
 
         def quantise(codes, scales, grouped):
@@ -124,24 +80,90 @@ def tile_deepgmm_pa_s_kernel(
                 in_=grouped[:].rearrange("p c t -> p (c t)"),
             )
 
-        wsig_grouped = keep.tile([P, X_DIM, PACK], BF16, align_bytes=64)
-        group(nc.vector.tensor_copy, wsig_grouped, wsig_raw)
-        wmu_grouped = keep.tile([P, X_DIM, PACK], BF16, align_bytes=64)
+        ident = keep.tile([P, P], F32)
+        masks.make_identity(nc, ident[:])
+        one_col = keep.tile([P, 1], F32)
+        nc.vector.memset(one_col[:], 1.0)
 
         y_codes = keep.tile([P, ROWS], U32, align_bytes=64)
         y_scales = keep.tile([P, ROWS], U8, align_bytes=64)
-        quantise(y_codes, y_scales, y_grouped)
         wsig_codes = keep.tile([P, X_DIM], U32, align_bytes=64)
         wsig_scales = keep.tile([P, X_DIM], U8, align_bytes=64)
-        quantise(wsig_codes, wsig_scales, wsig_grouped)
-        group(nc.vector.tensor_copy, wmu_grouped, wmu_raw)
+        wmu_raw = keep.tile([P, PACK, X_DIM], BF16)
+        logits = keep.tile([P, CLUSTERS], BF16)
+        params = keep.tile([P, DT, PARAM_ROWS], F32)
+
+        with tc.tile_pool(name="early", bufs=1) as early:
+            param_rows = early.tile([P, X_DIM], BF16)
+            nc.vector.memset(param_rows[:], 0.0)
+
+            y_sb = early.tile([P, NT, Y_DIM], BF16)
+            nc.sync.dma_start(out=y_sb[:], in_=Y.rearrange("(t p) k -> p t k", p=P))
+            wsig_raw = early.tile([P, PACK, X_DIM], BF16)
+            load_weight(wsig_raw, We_sig)
+            load_weight(wmu_raw, We_mu)
+            nc.sync.dma_start(out=logits[:], in_=phi_logits.partition_broadcast(P))
+
+            nc.scalar.dma_start(
+                out=param_rows[ROW_PHI_SIG : ROW_PHI_SIG + CLUSTERS, :], in_=phi_sigs
+            )
+            nc.scalar.dma_start(out=param_rows[ROW_PHI_MU : ROW_PHI_MU + CLUSTERS, :], in_=phi_mus)
+            nc.scalar.dma_start(
+                out=param_rows[ROW_BE_SIG : ROW_BE_SIG + 1, :],
+                in_=be_sig.rearrange("(o d) -> o d", o=1),
+            )
+            nc.scalar.dma_start(
+                out=param_rows[ROW_BE_MU : ROW_BE_MU + 1, :],
+                in_=be_mu.rearrange("(o d) -> o d", o=1),
+            )
+
+            warm = keep.tile([P, 1], F32)
+            nc.scalar.activation(out=warm[:], in_=one_col[:], func=ACT.Exp)
+
+            y_words = y_sb[:].bitcast(F32)
+            yT_ps = psum.tile([P, HALVES, ROWS], F32, tag="bank")
+            for nt in range(NT):
+                for u in range(HALVES):
+                    nc.tensor.transpose(
+                        yT_ps[:, u, nt * P : (nt + 1) * P],
+                        y_words[:, nt, u * P : (u + 1) * P],
+                        ident[:],
+                    )
+            y_grouped = early.tile([P, ROWS, PACK], BF16, align_bytes=64)
+            nc.vector.tensor_copy(
+                out=y_grouped[:].bitcast(F32), in_=yT_ps[:].rearrange("p u n -> p n u")
+            )
+
+            param_rows_f = early.tile([P, X_DIM], F32)
+            nc.scalar.copy(out=param_rows_f[:], in_=param_rows[:])
+            param_ps = psum.tile([P, DT, P], F32, tag="bank")
+            for dt in range(DT):
+                nc.tensor.transpose(
+                    param_ps[:, dt, :], param_rows_f[:, dt * P : (dt + 1) * P], ident[:]
+                )
+            nc.scalar.copy(out=params[:], in_=param_ps[:, :, 0:PARAM_ROWS])
+
+            wsig_grouped = early.tile([P, X_DIM, PACK], BF16, align_bytes=64)
+            group(wsig_grouped, wsig_raw)
+            quantise(y_codes, y_scales, y_grouped)
+            quantise(wsig_codes, wsig_scales, wsig_grouped)
+
+        work = ctx.enter_context(tc.tile_pool(name="work", bufs=3))
+        outs = ctx.enter_context(tc.tile_pool(name="outs", bufs=2 * NT))
+        diffs = ctx.enter_context(tc.tile_pool(name="diffs", bufs=VECTOR_REST))
+
+        def param(dt, row):
+            return params[:, dt, row : row + 1]
+
+        wmu_grouped = keep.tile([P, X_DIM, PACK], BF16, align_bytes=64)
+        group(wmu_grouped, wmu_raw)
 
         def project(w_codes, w_scales):
-            banks = []
-            for half in range(DT // 2):
-                acc = psum.tile([P, 2, ROWS], F32, tag="bank", name="acc")
-                for j in range(2):
-                    cols = slice((2 * half + j) * P, (2 * half + j + 1) * P)
+            results = []
+            for first in range(0, DT, TILES_PER_BANK):
+                acc = psum.tile([P, TILES_PER_BANK, ROWS], F32, tag="bank")
+                for j in range(TILES_PER_BANK):
+                    cols = slice((first + j) * P, (first + j + 1) * P)
                     nc.tensor.matmul_mx(
                         out=acc[:, j, :],
                         lhsT=w_codes[:, cols].bitcast(FP8X4),
@@ -151,31 +173,35 @@ def tile_deepgmm_pa_s_kernel(
                         start=True,
                         stop=True,
                     )
-                banks.append(acc)
-            return banks
+                    results.append(acc[:, j, :])
+            return results
 
-        sig_banks = project(wsig_codes, wsig_scales)
+        sig_acc = project(wsig_codes, wsig_scales)
         v = keep.tile([P, DT, ROWS], F32)
-        term = keep.tile([P, DT, ROWS], F32)
+        abs_v = keep.tile([P, DT, ROWS], F32)
+        exp_v = keep.tile([P, DT, ROWS], F32)
+        log_v = keep.tile([P, DT, ROWS], F32)
         for dt in range(DT):
             nc.vector.tensor_scalar(
-                out=v[:, dt, :], in0=sig_banks[dt // 2][:, dt % 2, :],
+                out=v[:, dt, :], in0=sig_acc[dt],
                 scalar1=param(dt, ROW_BE_SIG), scalar2=None, op0=ALU.add,
             )
-            nc.scalar.activation(out=term[:, dt, :], in_=v[:, dt, :], func=ACT.Abs)
+            nc.scalar.activation(out=abs_v[:, dt, :], in_=v[:, dt, :], func=ACT.Abs)
         for dt in range(DT):
-            nc.scalar.activation(out=term[:, dt, :], in_=term[:, dt, :], func=ACT.Exp, scale=-1.0)
+            nc.scalar.activation(out=exp_v[:, dt, :], in_=abs_v[:, dt, :], func=ACT.Exp, scale=-1.0)
         for dt in range(DT):
-            nc.scalar.activation(out=term[:, dt, :], in_=term[:, dt, :], func=ACT.Ln, bias=one_col[:])
+            nc.scalar.activation(
+                out=log_v[:, dt, :], in_=exp_v[:, dt, :], func=ACT.Ln, bias=one_col[:]
+            )
 
         wmu_codes = keep.tile([P, X_DIM], U32, align_bytes=64)
         wmu_scales = keep.tile([P, X_DIM], U8, align_bytes=64)
         quantise(wmu_codes, wmu_scales, wmu_grouped)
-        mu_banks = project(wmu_codes, wmu_scales)
+        mu_acc = project(wmu_codes, wmu_scales)
         muT = keep.tile([P, DT, ROWS], F32)
         for dt in range(DT):
             nc.vector.tensor_scalar(
-                out=muT[:, dt, :], in0=mu_banks[dt // 2][:, dt % 2, :],
+                out=muT[:, dt, :], in0=mu_acc[dt],
                 scalar1=param(dt, ROW_BE_MU), scalar2=None, op0=ALU.add,
             )
         relu_v = keep.tile([P, DT, ROWS], F32)
@@ -223,12 +249,12 @@ def tile_deepgmm_pa_s_kernel(
         sigT = keep.tile([P, DT, ROWS], F32)
         for dt in range(DT):
             nc.vector.scalar_tensor_tensor(
-                out=sigT[:, dt, :], in0=term[:, dt, :], scalar=1e-3, in1=relu_v[:, dt, :],
+                out=sigT[:, dt, :], in0=log_v[:, dt, :], scalar=SIG_FLOOR, in1=relu_v[:, dt, :],
                 op0=ALU.add, op1=ALU.add,
             )
 
         def rows_onto_partitions(src):
-            bank = psum.tile([P, X_DIM], F32, tag="bank", name="bank")
+            bank = psum.tile([P, X_DIM], F32, tag="bank")
             for dt in range(DT):
                 nc.tensor.transpose(bank[:, dt * P : (dt + 1) * P], src[:, dt, :], ident[:])
             return bank
@@ -252,7 +278,8 @@ def tile_deepgmm_pa_s_kernel(
                 )
             if k >= VECTOR_START:
                 square(nc.vector, k - VECTOR_START, diff)
-        rest = range(CLUSTERS - VECTOR_START, VECTOR_UNITS)
+
+        rest = range(VECTOR_UNITS - VECTOR_REST, VECTOR_UNITS)
         rest_diffs = [vector_difference(unit) for unit in rest]
         for unit, diff in zip(rest, rest_diffs):
             square(nc.vector, unit, diff)

@@ -26,7 +26,7 @@ DT = X_DIM // P
 
 PACK = 4
 PAIR = 2
-HALVES = PACK // PAIR
+K_HALVES = PACK // PAIR
 assert Y_DIM == P * PACK
 RUN = 4
 TILES_PER_BANK = BANK_F32 // ROWS
@@ -38,16 +38,16 @@ ROW_BE_SIG = 2 * CLUSTERS + 1
 PARAM_ROWS = 2 * CLUSTERS + 2
 
 VECTOR_CLUSTERS = 8
-SCALAR_CLUSTERS = 5
-HALF = DT // 2
-UNITS_PER_CLUSTER = DT // HALF
+SCALAR_CLUSTERS = 4
+UNIT_TILES = DT // 2
+UNITS_PER_CLUSTER = DT // UNIT_TILES
 VECTOR_UNITS = VECTOR_CLUSTERS * UNITS_PER_CLUSTER
 GPSIMD_FIRST_UNIT = (VECTOR_CLUSTERS + SCALAR_CLUSTERS) * UNITS_PER_CLUSTER
 ALL_UNITS = CLUSTERS * UNITS_PER_CLUSTER
 VECTOR_START = PSUM_BANKS // NT
 VECTOR_REST = VECTOR_UNITS - (CLUSTERS - VECTOR_START)
-SCALAR_UNITS = SCALAR_CLUSTERS * DT
-SCALAR_LEAD = SCALAR_UNITS // 2
+SCALAR_BLOCKS = SCALAR_CLUSTERS * DT
+SCALAR_LEAD = SCALAR_BLOCKS // 2
 
 FLOPS = 2 * 2 * ROWS * Y_DIM * X_DIM
 
@@ -63,8 +63,8 @@ def tile_deepgmm_pa_s_kernel(
 
         def load_weight(raw, w):
             nc.sync.dma_start(
-                out=raw[:].rearrange("p (u e) c -> p u (e c)", u=HALVES),
-                in_=w.rearrange("(u p e) c -> p u (e c)", u=HALVES, e=PAIR),
+                out=raw[:].rearrange("p (u e) c -> p u (e c)", u=K_HALVES),
+                in_=w.rearrange("(u p e) c -> p u (e c)", u=K_HALVES, e=PAIR),
             )
 
         def group(grouped, raw):
@@ -121,9 +121,9 @@ def tile_deepgmm_pa_s_kernel(
             nc.scalar.activation(out=warm[:], in_=one_col[:], func=ACT.Exp)
 
             y_words = y_sb[:].bitcast(F32)
-            yT_ps = psum.tile([P, HALVES, ROWS], F32, tag="bank")
+            yT_ps = psum.tile([P, K_HALVES, ROWS], F32, tag="bank")
             for nt in range(NT):
-                for u in range(HALVES):
+                for u in range(K_HALVES):
                     nc.tensor.transpose(
                         yT_ps[:, u, nt * P : (nt + 1) * P],
                         y_words[:, nt, u * P : (u + 1) * P],
@@ -210,10 +210,10 @@ def tile_deepgmm_pa_s_kernel(
         dist2 = keep.tile([P, CLUSTERS, DT, ROWS], F32)
 
         def vector_difference(unit):
-            k, half = divmod(unit, UNITS_PER_CLUSTER)
-            diff = diffs.tile([P, HALF, ROWS], F32)
-            for j in range(HALF):
-                dt = half * HALF + j
+            k, part = divmod(unit, UNITS_PER_CLUSTER)
+            diff = diffs.tile([P, UNIT_TILES, ROWS], F32)
+            for j in range(UNIT_TILES):
+                dt = part * UNIT_TILES + j
                 nc.vector.tensor_scalar(
                     out=diff[:, j, :], in0=muT[:, dt, :],
                     scalar1=param(dt, ROW_PHI_MU + k), scalar2=None, op0=ALU.subtract,
@@ -221,30 +221,30 @@ def tile_deepgmm_pa_s_kernel(
             return diff
 
         def square(engine, unit, diff):
-            k, half = divmod(unit, UNITS_PER_CLUSTER)
-            tiles = slice(half * HALF, (half + 1) * HALF)
+            k, part = divmod(unit, UNITS_PER_CLUSTER)
+            tiles = slice(part * UNIT_TILES, (part + 1) * UNIT_TILES)
             engine.tensor_tensor(out=dist2[:, k, tiles, :], in0=diff[:], in1=diff[:], op=ALU.mult)
 
         def gpsimd_square(unit):
-            k, half = divmod(unit, UNITS_PER_CLUSTER)
-            diff = diffs.tile([P, HALF, ROWS], F32)
-            for j in range(HALF):
-                dt = half * HALF + j
+            k, part = divmod(unit, UNITS_PER_CLUSTER)
+            diff = diffs.tile([P, UNIT_TILES, ROWS], F32)
+            for j in range(UNIT_TILES):
+                dt = part * UNIT_TILES + j
                 nc.gpsimd.tensor_scalar(
                     out=diff[:, j, :], in0=muT[:, dt, :],
                     scalar1=-1.0, scalar2=param(dt, ROW_PHI_MU + k), op0=ALU.mult, op1=ALU.add,
                 )
             square(nc.gpsimd, unit, diff)
 
-        def scalar_square(unit):
-            k, dt = divmod(VECTOR_CLUSTERS * DT + unit, DT)
+        def scalar_square(block):
+            k, dt = divmod(VECTOR_CLUSTERS * DT + block, DT)
             nc.scalar.activation(
                 out=dist2[:, k, dt, :], in_=muT[:, dt, :], func=ACT.Square,
                 scale=-1.0, bias=param(dt, ROW_PHI_MU + k),
             )
 
-        for unit in range(SCALAR_LEAD):
-            scalar_square(unit)
+        for block in range(SCALAR_LEAD):
+            scalar_square(block)
 
         sigT = keep.tile([P, DT, ROWS], F32)
         for dt in range(DT):
@@ -271,9 +271,9 @@ def tile_deepgmm_pa_s_kernel(
                     scalar1=param(dt, ROW_PHI_SIG + k), scalar2=None, op0=ALU.add,
                 )
             for nt in range(NT):
-                std = rows_onto_partitions(stdT[:, :, nt * P : (nt + 1) * P])
+                std_bank = rows_onto_partitions(stdT[:, :, nt * P : (nt + 1) * P])
                 nc.scalar.activation(
-                    out=ln_std[:, k, nt, :], in_=std[:], func=ACT.Ln,
+                    out=ln_std[:, k, nt, :], in_=std_bank[:], func=ACT.Ln,
                     accum_out=ln_sum[:, nt, k : k + 1],
                 )
             if k >= VECTOR_START:
@@ -296,13 +296,13 @@ def tile_deepgmm_pa_s_kernel(
         for k in range(CLUSTERS):
             inv_var = work.tile([P, NT, X_DIM], F32)
             nc.scalar.activation(out=inv_var[:], in_=ln_std[:, k, :, :], func=ACT.Exp, scale=-2.0)
-            if SCALAR_LEAD + k < SCALAR_UNITS:
+            if SCALAR_LEAD + k < SCALAR_BLOCKS:
                 scalar_square(SCALAR_LEAD + k)
             for nt in range(NT):
-                d2 = rows_onto_partitions(dist2[:, k, :, nt * P : (nt + 1) * P])
+                dist2_bank = rows_onto_partitions(dist2[:, k, :, nt * P : (nt + 1) * P])
                 product = work.tile([P, X_DIM], F32)
                 nc.vector.scalar_tensor_tensor(
-                    out=product[:], in0=d2[:], scalar=0.5, in1=inv_var[:, nt, :],
+                    out=product[:], in0=dist2_bank[:], scalar=0.5, in1=inv_var[:, nt, :],
                     op0=ALU.mult, op1=ALU.mult, accum_out=maha_sum[:, nt, k : k + 1],
                 )
 

from contextlib import ExitStack

import concourse.masks as masks
import concourse.mybir as mybir

F32 = mybir.dt.float32
BF16 = mybir.dt.bfloat16
U32 = mybir.dt.uint32
U8 = mybir.dt.uint8
FP8X4 = mybir.dt.float8_e4m3fn_x4
ACT = mybir.ActivationFunctionType
ALU = mybir.AluOpType
AXIS = mybir.AxisListType

P = 128
PSUM_BANKS = 8
BANK_F32 = 512

ROWS = 256
Y_DIM = 512
X_DIM = 512
CLUSTERS = 16
SIG_FLOOR = 1e-3
NT = ROWS // P
DT = X_DIM // P

PACK = 4
PAIR = 2
K_HALVES = PACK // PAIR
assert Y_DIM == P * PACK
RUN = 4
TILES_PER_BANK = BANK_F32 // ROWS

ROW_PHI_MU = 0
ROW_PHI_SIG = CLUSTERS
ROW_BE_MU = 2 * CLUSTERS
ROW_BE_SIG = 2 * CLUSTERS + 1
PARAM_ROWS = 2 * CLUSTERS + 2

VECTOR_CLUSTERS = 8
SCALAR_CLUSTERS = 4
UNIT_TILES = DT // 2
UNITS_PER_CLUSTER = DT // UNIT_TILES
VECTOR_UNITS = VECTOR_CLUSTERS * UNITS_PER_CLUSTER
GPSIMD_FIRST_UNIT = (VECTOR_CLUSTERS + SCALAR_CLUSTERS) * UNITS_PER_CLUSTER
ALL_UNITS = CLUSTERS * UNITS_PER_CLUSTER
VECTOR_START = PSUM_BANKS // NT
VECTOR_REST = VECTOR_UNITS - (CLUSTERS - VECTOR_START)
SCALAR_BLOCKS = SCALAR_CLUSTERS * DT
SCALAR_LEAD = SCALAR_BLOCKS // 2

FLOPS = 2 * 2 * ROWS * Y_DIM * X_DIM


def tile_deepgmm_pa_s_kernel(
    tc, Y, We_mu, be_mu, We_sig, be_sig, phi_mus, phi_sigs, phi_logits, out_0, out_1, out_2
):
    nc = tc.nc
    with ExitStack() as ctx:
        keep = ctx.enter_context(tc.tile_pool(name="keep", bufs=1))
        psum = ctx.enter_context(tc.psum_pool(name="psum", bufs=PSUM_BANKS))
        ctx.enter_context(tc.manual_schedule())

        def load_weight(raw, w):
            nc.sync.dma_start(
                out=raw[:].rearrange("p (u e) c -> p u (e c)", u=K_HALVES),
                in_=w.rearrange("(u p e) c -> p u (e c)", u=K_HALVES, e=PAIR),
            )

        def group(grouped, raw):
            nc.vector.tensor_copy(
                out=grouped[:].rearrange("p (c i) t -> p c t i", i=RUN),
                in_=raw[:].rearrange("p t (c i) -> p c t i", i=RUN),
            )

        def quantise(codes, scales, grouped):
            nc.vector.quantize_mx(
                out=codes[:].bitcast(FP8X4),
                scales=scales[:],
                in_=grouped[:].rearrange("p c t -> p (c t)"),
            )

        ident = keep.tile([P, P], F32)
        masks.make_identity(nc, ident[:])
        one_col = keep.tile([P, 1], F32)
        nc.vector.memset(one_col[:], 1.0)

        y_codes = keep.tile([P, ROWS], U32, align_bytes=64)
        y_scales = keep.tile([P, ROWS], U8, align_bytes=64)
        wsig_codes = keep.tile([P, X_DIM], U32, align_bytes=64)
        wsig_scales = keep.tile([P, X_DIM], U8, align_bytes=64)
        wmu_raw = keep.tile([P, PACK, X_DIM], BF16)
        logits = keep.tile([P, CLUSTERS], BF16)
        params = keep.tile([P, DT, PARAM_ROWS], F32)

        with tc.tile_pool(name="early", bufs=1) as early:
            param_rows = early.tile([P, X_DIM], BF16)
            nc.vector.memset(param_rows[:], 0.0)

            y_sb = early.tile([P, NT, Y_DIM], BF16)
            nc.sync.dma_start(out=y_sb[:], in_=Y.rearrange("(t p) k -> p t k", p=P))
            wsig_raw = early.tile([P, PACK, X_DIM], BF16)
            load_weight(wsig_raw, We_sig)
            load_weight(wmu_raw, We_mu)
            nc.sync.dma_start(out=logits[:], in_=phi_logits.partition_broadcast(P))

            nc.scalar.dma_start(
                out=param_rows[ROW_PHI_SIG : ROW_PHI_SIG + CLUSTERS, :], in_=phi_sigs
            )
            nc.scalar.dma_start(out=param_rows[ROW_PHI_MU : ROW_PHI_MU + CLUSTERS, :], in_=phi_mus)
            nc.scalar.dma_start(
                out=param_rows[ROW_BE_SIG : ROW_BE_SIG + 1, :],
                in_=be_sig.rearrange("(o d) -> o d", o=1),
            )
            nc.scalar.dma_start(
                out=param_rows[ROW_BE_MU : ROW_BE_MU + 1, :],
                in_=be_mu.rearrange("(o d) -> o d", o=1),
            )

            warm = keep.tile([P, 1], F32)
            nc.scalar.activation(out=warm[:], in_=one_col[:], func=ACT.Exp)

            y_words = y_sb[:].bitcast(F32)
            yT_ps = psum.tile([P, K_HALVES, ROWS], F32, tag="bank")
            for nt in range(NT):
                for u in range(K_HALVES):
                    nc.tensor.transpose(
                        yT_ps[:, u, nt * P : (nt + 1) * P],
                        y_words[:, nt, u * P : (u + 1) * P],
                        ident[:],
                    )
            y_grouped = early.tile([P, ROWS, PACK], BF16, align_bytes=64)
            nc.vector.tensor_copy(
                out=y_grouped[:].bitcast(F32), in_=yT_ps[:].rearrange("p u n -> p n u")
            )

            param_rows_f = early.tile([P, X_DIM], F32)
            nc.scalar.copy(out=param_rows_f[:], in_=param_rows[:])
            param_ps = psum.tile([P, DT, P], F32, tag="bank")
            for dt in range(DT):
                nc.tensor.transpose(
                    param_ps[:, dt, :], param_rows_f[:, dt * P : (dt + 1) * P], ident[:]
                )
            nc.scalar.copy(out=params[:], in_=param_ps[:, :, 0:PARAM_ROWS])

            wsig_grouped = early.tile([P, X_DIM, PACK], BF16, align_bytes=64)
            group(wsig_grouped, wsig_raw)
            quantise(y_codes, y_scales, y_grouped)
            quantise(wsig_codes, wsig_scales, wsig_grouped)

        work = ctx.enter_context(tc.tile_pool(name="work", bufs=3))
        outs = ctx.enter_context(tc.tile_pool(name="outs", bufs=2 * NT))
        diffs = ctx.enter_context(tc.tile_pool(name="diffs", bufs=VECTOR_REST))

        def param(dt, row):
            return params[:, dt, row : row + 1]

        wmu_grouped = keep.tile([P, X_DIM, PACK], BF16, align_bytes=64)
        group(wmu_grouped, wmu_raw)

        def project(w_codes, w_scales):
            results = []
            for first in range(0, DT, TILES_PER_BANK):
                acc = psum.tile([P, TILES_PER_BANK, ROWS], F32, tag="bank")
                for j in range(TILES_PER_BANK):
                    cols = slice((first + j) * P, (first + j + 1) * P)
                    nc.tensor.matmul_mx(
                        out=acc[:, j, :],
                        lhsT=w_codes[:, cols].bitcast(FP8X4),
                        lhsT_scale=w_scales[:, cols],
                        rhs=y_codes[:].bitcast(FP8X4),
                        rhs_scale=y_scales[:],
                        start=True,
                        stop=True,
                    )
                    results.append(acc[:, j, :])
            return results

        sig_acc = project(wsig_codes, wsig_scales)
        v = keep.tile([P, DT, ROWS], F32)
        abs_v = keep.tile([P, DT, ROWS], F32)
        exp_v = keep.tile([P, DT, ROWS], F32)
        log_v = keep.tile([P, DT, ROWS], F32)
        for dt in range(DT):
            nc.vector.tensor_scalar(
                out=v[:, dt, :], in0=sig_acc[dt],
                scalar1=param(dt, ROW_BE_SIG), scalar2=None, op0=ALU.add,
            )
            nc.scalar.activation(out=abs_v[:, dt, :], in_=v[:, dt, :], func=ACT.Abs)
        for dt in range(DT):
            nc.scalar.activation(out=exp_v[:, dt, :], in_=abs_v[:, dt, :], func=ACT.Exp, scale=-1.0)
        for dt in range(DT):
            nc.scalar.activation(
                out=log_v[:, dt, :], in_=exp_v[:, dt, :], func=ACT.Ln, bias=one_col[:]
            )

        wmu_codes = keep.tile([P, X_DIM], U32, align_bytes=64)
        wmu_scales = keep.tile([P, X_DIM], U8, align_bytes=64)
        quantise(wmu_codes, wmu_scales, wmu_grouped)
        mu_acc = project(wmu_codes, wmu_scales)
        muT = keep.tile([P, DT, ROWS], F32)
        for dt in range(DT):
            nc.vector.tensor_scalar(
                out=muT[:, dt, :], in0=mu_acc[dt],
                scalar1=param(dt, ROW_BE_MU), scalar2=None, op0=ALU.add,
            )
        relu_v = keep.tile([P, DT, ROWS], F32)
        nc.vector.tensor_scalar_max(out=relu_v[:], in0=v[:], scalar1=0.0)

        dist2 = keep.tile([P, CLUSTERS, DT, ROWS], F32)

        def vector_difference(unit):
            k, part = divmod(unit, UNITS_PER_CLUSTER)
            diff = diffs.tile([P, UNIT_TILES, ROWS], F32)
            for j in range(UNIT_TILES):
                dt = part * UNIT_TILES + j
                nc.vector.tensor_scalar(
                    out=diff[:, j, :], in0=muT[:, dt, :],
                    scalar1=param(dt, ROW_PHI_MU + k), scalar2=None, op0=ALU.subtract,
                )
            return diff

        def square(engine, unit, diff):
            k, part = divmod(unit, UNITS_PER_CLUSTER)
            tiles = slice(part * UNIT_TILES, (part + 1) * UNIT_TILES)
            engine.tensor_tensor(out=dist2[:, k, tiles, :], in0=diff[:], in1=diff[:], op=ALU.mult)

        def gpsimd_square(unit):
            k, part = divmod(unit, UNITS_PER_CLUSTER)
            diff = diffs.tile([P, UNIT_TILES, ROWS], F32)
            for j in range(UNIT_TILES):
                dt = part * UNIT_TILES + j
                nc.gpsimd.tensor_scalar(
                    out=diff[:, j, :], in0=muT[:, dt, :],
                    scalar1=-1.0, scalar2=param(dt, ROW_PHI_MU + k), op0=ALU.mult, op1=ALU.add,
                )
            square(nc.gpsimd, unit, diff)

        def scalar_square(block):
            k, dt = divmod(VECTOR_CLUSTERS * DT + block, DT)
            nc.scalar.activation(
                out=dist2[:, k, dt, :], in_=muT[:, dt, :], func=ACT.Square,
                scale=-1.0, bias=param(dt, ROW_PHI_MU + k),
            )

        for block in range(SCALAR_LEAD):
            scalar_square(block)

        sigT = keep.tile([P, DT, ROWS], F32)
        for dt in range(DT):
            nc.vector.scalar_tensor_tensor(
                out=sigT[:, dt, :], in0=log_v[:, dt, :], scalar=SIG_FLOOR, in1=relu_v[:, dt, :],
                op0=ALU.add, op1=ALU.add,
            )

        def rows_onto_partitions(src):
            bank = psum.tile([P, X_DIM], F32, tag="bank")
            for dt in range(DT):
                nc.tensor.transpose(bank[:, dt * P : (dt + 1) * P], src[:, dt, :], ident[:])
            return bank

        ln_std = keep.tile([P, CLUSTERS, NT, X_DIM], F32)
        ln_sum = keep.tile([P, NT, CLUSTERS], F32)
        for k in range(CLUSTERS):
            if k >= VECTOR_START:
                diff = vector_difference(k - VECTOR_START)
            stdT = work.tile([P, DT, ROWS], F32)
            for dt in range(DT):
                nc.vector.tensor_scalar(
                    out=stdT[:, dt, :], in0=sigT[:, dt, :],
                    scalar1=param(dt, ROW_PHI_SIG + k), scalar2=None, op0=ALU.add,
                )
            for nt in range(NT):
                std_bank = rows_onto_partitions(stdT[:, :, nt * P : (nt + 1) * P])
                nc.scalar.activation(
                    out=ln_std[:, k, nt, :], in_=std_bank[:], func=ACT.Ln,
                    accum_out=ln_sum[:, nt, k : k + 1],
                )
            if k >= VECTOR_START:
                square(nc.vector, k - VECTOR_START, diff)

        rest = range(VECTOR_UNITS - VECTOR_REST, VECTOR_UNITS)
        rest_diffs = [vector_difference(unit) for unit in rest]
        for unit, diff in zip(rest, rest_diffs):
            square(nc.vector, unit, diff)
        for unit in range(GPSIMD_FIRST_UNIT, ALL_UNITS):
            gpsimd_square(unit)

        base = keep.tile([P, NT, CLUSTERS], F32)
        nc.vector.tensor_tensor(
            out=base[:], in0=logits[:].unsqueeze(1).to_broadcast([P, NT, CLUSTERS]), in1=ln_sum[:],
            op=ALU.subtract,
        )

        maha_sum = keep.tile([P, NT, CLUSTERS], F32)
        for k in range(CLUSTERS):
            inv_var = work.tile([P, NT, X_DIM], F32)
            nc.scalar.activation(out=inv_var[:], in_=ln_std[:, k, :, :], func=ACT.Exp, scale=-2.0)
            if SCALAR_LEAD + k < SCALAR_BLOCKS:
                scalar_square(SCALAR_LEAD + k)
            for nt in range(NT):
                dist2_bank = rows_onto_partitions(dist2[:, k, :, nt * P : (nt + 1) * P])
                product = work.tile([P, X_DIM], F32)
                nc.vector.scalar_tensor_tensor(
                    out=product[:], in0=dist2_bank[:], scalar=0.5, in1=inv_var[:, nt, :],
                    op0=ALU.mult, op1=ALU.mult, accum_out=maha_sum[:, nt, k : k + 1],
                )

        def store_rows(copy, dram, src):
            for nt in range(NT):
                bank = rows_onto_partitions(src[:, :, nt * P : (nt + 1) * P])
                rows_sb = outs.tile([P, X_DIM], F32)
                copy(out=rows_sb[:], in_=bank[:])
                nc.sync.dma_start(out=dram[nt * P : (nt + 1) * P, :], in_=rows_sb[:])

        store_rows(nc.scalar.copy, out_0, muT)

        z = keep.tile([P, NT, CLUSTERS], F32)
        nc.vector.tensor_tensor(out=z[:], in0=base[:], in1=maha_sum[:], op=ALU.subtract)
        z_max = keep.tile([P, NT], F32)
        nc.vector.tensor_reduce(out=z_max[:], in_=z[:], axis=AXIS.X, op=ALU.max)
        z_shift = keep.tile([P, NT, CLUSTERS], F32)
        nc.vector.tensor_tensor(
            out=z_shift[:], in0=z[:], in1=z_max[:].unsqueeze(2).to_broadcast([P, NT, CLUSTERS]),
            op=ALU.subtract,
        )
        exp_z = keep.tile([P, NT, CLUSTERS], F32)
        exp_sum = keep.tile([P, NT], F32)
        for nt in range(NT):
            nc.scalar.activation(
                out=exp_z[:, nt, :], in_=z_shift[:, nt, :], func=ACT.Exp,
                accum_out=exp_sum[:, nt : nt + 1],
            )
        log_sum = keep.tile([P, NT], F32)
        nc.scalar.activation(out=log_sum[:], in_=exp_sum[:], func=ACT.Ln)

        store_rows(nc.vector.tensor_copy, out_1, sigT)

        z_log_probs = keep.tile([P, NT, CLUSTERS], F32)
        nc.vector.tensor_tensor(
            out=z_log_probs[:], in0=z_shift[:],
            in1=log_sum[:].unsqueeze(2).to_broadcast([P, NT, CLUSTERS]), op=ALU.subtract,
        )
        nc.sync.dma_start(out=out_2.rearrange("(t p) k -> p t k", p=P), in_=z_log_probs[:])
